import numpy as np
import ml_dtypes


BF16 = ml_dtypes.bfloat16


def bf(x):
    return np.asarray(x, np.float32).astype(BF16)


def f64(x):
    return np.asarray(x).astype(np.float64)


E2M1 = np.array([0.0, 0.5, 1.0, 1.5, 2.0, 3.0, 4.0, 6.0, -0.0, -0.5, -1.0, -1.5, -2.0, -3.0, -4.0, -6.0])


def pack_weight(w, fmt):
    k, n = w.shape
    w = f64(bf(w)).reshape(k // 32, 32, n)
    amax = np.abs(w).max(1)
    if fmt == "e4m3":
        byte = np.frexp(amax)[1] - 1 + 127 - 7
    else:
        mant, ex = np.frexp(amax / 6.0)
        byte = np.where(mant > 0.5, ex, ex - 1) + 127
    byte = np.clip(np.where(amax > 0, byte, 1), 1, 254)
    scaled = (w * np.exp2(127.0 - byte)[:, None, :]).reshape(k, n).astype(np.float32)
    by_word = np.ascontiguousarray(scaled.reshape(k // 512, 128, 4, n).transpose(0, 1, 3, 2))
    if fmt == "e4m3":
        words = by_word.astype(ml_dtypes.float8_e4m3fn).view(np.uint8)
    else:
        c = by_word.astype(ml_dtypes.float4_e2m1fn).view(np.uint8) & 0xF
        words = c[..., 0::2] | (c[..., 1::2] << 4)
    return np.ascontiguousarray(words), np.ascontiguousarray(byte.astype(np.uint8).reshape(k // 512, 16, n))


def unpack_weight(words, scales, fmt):
    g, p, n, _ = words.shape
    if fmt == "e4m3":
        vals = np.ascontiguousarray(words).view(ml_dtypes.float8_e4m3fn).astype(np.float64)
    else:
        nib = np.empty((g, p, n, 4), np.uint8)
        nib[..., 0::2] = words & 0xF
        nib[..., 1::2] = words >> 4
        vals = E2M1[nib]
    vals = vals * np.repeat(np.exp2(scales.astype(np.float64) - 127.0), 8, axis=1)[..., None]
    return vals.transpose(0, 1, 3, 2).reshape(g * 512, n)

def pack4(w):
    words, scales = pack_weight(w, "e2m1")
    return words.reshape(words.shape[0], 128, -1), scales


def unpack4(words, scales):
    return unpack_weight(words.reshape(words.shape[0], 128, -1, 2), scales, "e2m1")


def kspread(k):
    return np.exp2(np.repeat(np.random.randint(-6, 7, k // 32), 32).astype(np.float64))


B, S, D, DM, DK = 2, 512, 1536, 1536, 64
LN_EPS = 1e-5


def setup_inputs():
    s = kspread(DM)
    h_attn = np.random.standard_normal((B, S, DM)) * 0.3 * s
    h_attn_words, h_attn_scales = pack4(h_attn.reshape(B * S, DM).T)
    Wo_words, Wo_scales = pack4(np.random.standard_normal((DM, D)) * 3.0 / np.sqrt(DM) / s[:, None])
    return {
        "h_attn_words": h_attn_words,
        "h_attn_scales": h_attn_scales,
        "Wo_words": Wo_words,
        "Wo_scales": Wo_scales,
        "bo": bf(np.random.standard_normal((B, S, D)) * 0.5 + np.random.uniform(0.25, 0.75, (B, 1, 1))),
        "x": bf(np.random.standard_normal((B, S, D))),
        "gamma": bf(1.0 + 0.1 * np.random.standard_normal((S, D))),
        "beta": bf(0.1 * np.random.standard_normal((S, D))),
    }


def reference(h_attn_words, h_attn_scales, Wo_words, Wo_scales, bo, x, gamma, beta):
    o = (unpack4(h_attn_words, h_attn_scales).T.reshape(B, S, DM) @ unpack4(Wo_words, Wo_scales)) + f64(bo)
    o = o + f64(x)
    mu = o.mean(axis=(-2, -1), keepdims=True)
    var = np.square(o - mu).mean(axis=(-2, -1), keepdims=True)
    return (o - mu) / np.sqrt(var + LN_EPS) * f64(gamma) + f64(beta)

@@ -1,0 +1,293 @@
+from contextlib import ExitStack
+
+import concourse.mybir as mybir
+from concourse.masks import make_identity
+
+F32 = mybir.dt.float32
+BF16 = mybir.dt.bfloat16
+U8 = mybir.dt.uint8
+I32 = mybir.dt.int32
+FP4X4 = mybir.dt.float4_e2m1fn_x4
+ALU = mybir.AluOpType
+ACT = mybir.ActivationFunctionType
+
+P = 128
+TOKENS = 1024
+D = 1536
+K = 1536
+PASSES = K // 512
+CHUNK = 512
+NCH = D // CHUNK
+TILES = TOKENS // P
+TPB = TILES // 2
+UNITS = TPB * NCH
+N_NORM = 512 * D
+LN_EPS = 1e-5
+FLOPS = 2 * TOKENS * D * K
+
+VUNITS = (1, 3, 4, 5, 10, 11, 15, 16, 17)
+GSL = ((3, 0, 1536), (2, 1024, 1536))
+LOADS = (0, "w1", "w2", 1, 2, 3, 4, "h1", 5, 6, 7)
+GB = (3, 2, 0, 1)
+RING = 7
+AHEAD = 1
+TOT0 = 1
+RECIP0 = 2
+WARM = 0
+
+
+def tile_multiheadattn_pb_kernel(
+    tc, h_attn_words, h_attn_scales, Wo_words, Wo_scales, bo, x, gamma, beta, out
+):
+    nc = tc.nc
+    bo_v = bo.flatten_outer_dims().rearrange("(i p) d -> i p d", p=P)
+    x_v = x.flatten_outer_dims().rearrange("(i p) d -> i p d", p=P)
+    out_v = out.flatten_outer_dims().rearrange("(i p) d -> i p d", p=P)
+    gamma_v = gamma.rearrange("(s p) d -> s p d", p=P)
+    beta_v = beta.rearrange("(s p) d -> s p d", p=P)
+
+    def cols(c):
+        return slice(c * CHUNK, (c + 1) * CHUNK)
+
+    with ExitStack() as ctx:
+        keep = ctx.enter_context(tc.tile_pool(name="keep", bufs=1))
+        ring = ctx.enter_context(tc.psum_pool(name="ring", bufs=RING))
+        tiny = ctx.enter_context(tc.psum_pool(name="tiny", bufs=1))
+        ctx.enter_context(tc.manual_schedule())
+
+        h_codes = [keep.tile([P, PASSES, TOKENS], U8, name="h_codes%d" % b, align_bytes=64) for b in range(2)]
+        h_planes = [keep.tile([P, PASSES, TOKENS // 2], U8, name="h_planes%d" % b, align_bytes=64) for b in range(2)]
+        w_codes = [keep.tile([P, PASSES, 2 * CHUNK], U8, name="w_codes%d" % c, align_bytes=64) for c in range(NCH)]
+        w_planes = keep.tile([P, PASSES, D], U8, name="w_planes", align_bytes=64)
+        bo_t = [keep.tile([P, D], BF16, name="bo_t%d" % i) for i in range(TILES)]
+        x_t = [keep.tile([P, D], BF16, name="x_t%d" % i) for i in range(TILES)]
+        gam = [keep.tile([P, D], BF16, name="gam%d" % s) for s in range(TPB)]
+        bet = [keep.tile([P, D], BF16, name="bet%d" % s) for s in range(TPB)]
+        o = [keep.tile([P, D], F32, name="o%d" % i) for i in range(TILES)]
+        ident = keep.tile([P, P], BF16, name="ident")
+        ones = keep.tile([P, P], F32, name="ones")
+        eps_t = keep.tile([P, 1], F32, name="eps_t")
+        warm = keep.tile([P, 1], F32, name="warm")
+        junk = keep.tile([P, CHUNK], BF16, name="junk")
+        junk_s = keep.tile([P, 2 * UNITS], F32, name="junk_s")
+        stat = [keep.tile([P, 2 * UNITS], F32, name="stat%d" % b) for b in range(2)]
+        negc = [keep.tile([P, 1], F32, name="negc%d" % b) for b in range(2)]
+        nmean = [keep.tile([P, 1], F32, name="nmean%d" % b) for b in range(2)]
+        qq = [keep.tile([P, 1], F32, name="qq%d" % b) for b in range(2)]
+        d2 = [keep.tile([P, 1], F32, name="d2%d" % b) for b in range(2)]
+        var = [keep.tile([P, 1], F32, name="var%d" % b) for b in range(2)]
+        std = [keep.tile([P, 1], F32, name="std%d" % b) for b in range(2)]
+        rstd = [keep.tile([P, 1], F32, name="rstd%d" % b) for b in range(2)]
+        nmr = [keep.tile([P, 1], F32, name="nmr%d" % b) for b in range(2)]
+
+        nc.vector.memset(h_planes[0][:].bitcast(I32), 0)
+        nc.vector.memset(w_planes[:].bitcast(I32), 0)
+        nc.vector.memset(eps_t[:], LN_EPS)
+        nc.vector.memset(ones[:], 1.0)
+        nc.vector.memset(h_planes[1][:].bitcast(I32), 0)
+        nc.scalar.activation(out=warm[:], in_=eps_t[:], func=ACT.Sqrt)
+        make_identity(nc, ident[:])
+
+        def load_codes(dst, src, lo, hi):
+            nc.sync.dma_start(
+                out=dst[:].bitcast(I32),
+                in_=src[:, :, lo:hi].rearrange("g p n -> p g n").bitcast(I32),
+            )
+
+        def load_planes(dst, src, lo, hi):
+            for q in range(4):
+                nc.sync.dma_start(
+                    out=dst[32 * q : 32 * q + 4, :, :].bitcast(I32),
+                    in_=src[:, 4 * q : 4 * q + 4, lo:hi].rearrange("g r n -> r g n").bitcast(I32),
+                )
+
+        def load_pair(i):
+            nc.sync.dma_start(out=bo_t[i][:], in_=bo_v[i])
+            nc.sync.dma_start(out=x_t[i][:], in_=x_v[i])
+
+        load_codes(h_codes[0], h_attn_words, 0, TOKENS)
+        load_codes(w_codes[0], Wo_words, 0, 2 * CHUNK)
+        load_planes(h_planes[0], h_attn_scales, 0, TOKENS // 2)
+        load_planes(w_planes, Wo_scales, 0, D)
+        for what in LOADS:
+            if what == "w1":
+                load_codes(w_codes[1], Wo_words, 2 * CHUNK, 4 * CHUNK)
+            elif what == "w2":
+                load_codes(w_codes[2], Wo_words, 4 * CHUNK, 6 * CHUNK)
+            elif what == "h1":
+                load_codes(h_codes[1], h_attn_words, TOKENS, 2 * TOKENS)
+                load_planes(h_planes[1], h_attn_scales, TOKENS // 2, TOKENS)
+            else:
+                load_pair(what)
+        for s in GB:
+            nc.sync.dma_start(out=gam[s][:], in_=gamma_v[s])
+            nc.sync.dma_start(out=bet[s][:], in_=beta_v[s])
+
+        for i in range(TILES):
+            runs = []
+            for c in range(NCH):
+                if i * NCH + c in VUNITS:
+                    continue
+                if runs and runs[-1][1] == c and i > 0:
+                    runs[-1][1] = c + 1
+                else:
+                    runs.append([c, c + 1])
+            for lo, hi in runs:
+                sl = slice(lo * CHUNK, hi * CHUNK)
+                nc.gpsimd.tensor_tensor(out=o[i][:, sl], in0=bo_t[i][:, sl], in1=x_t[i][:, sl], op=ALU.add)
+
+        acc = {}
+        xst = {}
+        NU = TILES * NCH
+
+        def stage(src, c):
+            st = ring.tile([P, CHUNK], F32, name="st", tag="bank")
+            nc.tensor.matmul(out=st[:], lhsT=ident[:], rhs=src[:, cols(c)], start=True, stop=True)
+            return st
+
+        def pe_unit(u):
+            i, c = u // NCH, u % NCH
+            b, s = i // TPB, i % TPB
+            a = ring.tile([P, CHUNK], F32, name="acc", tag="bank")
+            for g in range(PASSES):
+                nc.tensor.matmul_mx(
+                    out=a[:],
+                    lhsT=h_codes[b][:, g, 2 * P * s : 2 * P * (s + 1)].bitcast(FP4X4),
+                    lhsT_scale=h_planes[b][:, g, P * s : P * (s + 1)],
+                    rhs=w_codes[c][:, g, :].bitcast(FP4X4),
+                    rhs_scale=w_planes[:, g, cols(c)],
+                    start=(g == 0),
+                    stop=(g == PASSES - 1),
+                )
+            acc[u] = a
+
+        def sum_col(u):
+            return stat[u // UNITS][:, u % UNITS : u % UNITS + 1]
+
+        def v_first(u):
+            i, c = u // NCH, u % NCH
+            if u in VUNITS:
+                nc.vector.tensor_tensor(out=o[i][:, cols(c)], in0=acc[u][:], in1=bo_t[i][:, cols(c)], op=ALU.add)
+            else:
+                nc.vector.scalar_tensor_tensor(
+                    out=o[i][:, cols(c)], in0=acc[u][:], scalar=1.0, in1=o[i][:, cols(c)],
+                    op0=ALU.mult, op1=ALU.add, accum_out=sum_col(u),
+                )
+
+        def v_second(u):
+            i, c = u // NCH, u % NCH
+            nc.vector.scalar_tensor_tensor(
+                out=o[i][:, cols(c)], in0=o[i][:, cols(c)], scalar=1.0, in1=xst[u][:],
+                op0=ALU.mult, op1=ALU.add, accum_out=sum_col(u),
+            )
+
+        def shift(b):
+            t = tiny.tile([P, 1], F32, name="cs", tag="tiny")
+            nc.tensor.matmul(out=t[:], lhsT=ones[:], rhs=stat[b][:, 0:1], start=True, stop=True)
+            nc.scalar.activation(out=negc[b][:], in_=t[:], func=ACT.Copy, scale=-1.0 / (P * CHUNK))
+
+        def s_unit(u):
+            i, c = u // NCH, u % NCH
+            b = u // UNITS
+            j = UNITS + u % UNITS
+            nc.scalar.activation(
+                out=junk[:], in_=o[i][:, cols(c)], func=ACT.Square, bias=negc[b][:, 0:1], scale=1.0,
+                accum_out=stat[b][:, j : j + 1],
+            )
+
+        def chain_a(b):
+            t = tiny.tile([P, 2 * UNITS], F32, name="tot", tag="tiny")
+            nc.tensor.matmul(out=t[:], lhsT=ones[:], rhs=stat[b][:], start=True, stop=True)
+            nc.scalar.activation(out=junk_s[:, 0:UNITS], in_=t[:, 0:UNITS], func=ACT.Copy,
+                                 scale=-1.0 / N_NORM, accum_out=nmean[b][:])
+            nc.scalar.activation(out=junk_s[:, UNITS : 2 * UNITS], in_=t[:, UNITS : 2 * UNITS], func=ACT.Copy,
+                                 scale=1.0 / N_NORM, accum_out=qq[b][:])
+            nc.scalar.activation(out=d2[b][:], in_=nmean[b][:], func=ACT.Square, bias=negc[b][:, 0:1], scale=-1.0)
+            nc.scalar.activation(out=var[b][:], in_=d2[b][:], func=ACT.Identity, bias=qq[b][:, 0:1], scale=-1.0)
+            nc.scalar.activation(out=std[b][:], in_=var[b][:], func=ACT.Sqrt, bias=eps_t[:, 0:1], scale=1.0)
+
+        def chain_b(b):
+            nc.vector.reciprocal(out=rstd[b][:], in_=std[b][:])
+            nc.scalar.activation(out=nmr[b][:], in_=nmean[b][:], func=ACT.Copy, scale=rstd[b][:, 0:1])
+
+        def g_phase2(b):
+            for s, lo, hi in GSL:
+                t = o[b * TPB + s]
+                nc.scalar.activation(out=t[:, lo:hi], in_=t[:, lo:hi], func=ACT.Identity, bias=nmr[b][:, 0:1], scale=rstd[b][:, 0:1])
+                nc.gpsimd.tensor_tensor(out=t[:, lo:hi], in0=t[:, lo:hi], in1=gam[s][:, lo:hi], op=ALU.mult)
+                nc.gpsimd.tensor_tensor(out=t[:, lo:hi], in0=t[:, lo:hi], in1=bet[s][:, lo:hi], op=ALU.add)
+
+        for w in range(WARM):
+            wt = ring.tile([P, CHUNK], F32, name="wt", tag="bank")
+            nc.tensor.matmul(out=wt[:, 0:P], lhsT=ident[:], rhs=ident[:], start=True, stop=True)
+
+        for u in range(-AHEAD, NU + 2):
+            if u + AHEAD < NU:
+                pe_unit(u + AHEAD)
+            if 0 <= u + AHEAD - 1 < NU and u + AHEAD - 1 in VUNITS:
+                xst[u + AHEAD - 1] = stage(x_t[(u + AHEAD - 1) // NCH], (u + AHEAD - 1) % NCH)
+            if 0 <= u < NU:
+                v_first(u)
+            if 0 <= u - 1 < NU and u - 1 in VUNITS:
+                v_second(u - 1)
+            if u - 1 in (0, UNITS):
+                shift((u - 1) // UNITS)
+            if u - 2 == UNITS - 1 + TOT0:
+                chain_a(0)
+            if u - 2 == UNITS - 1 + RECIP0:
+                chain_b(0)
+                g_phase2(0)
+            if 0 <= u - 2 < NU:
+                s_unit(u - 2)
+
+        gpos = [(s, c) for s, lo, hi in GSL for c in range(lo // CHUNK, hi // CHUNK)]
+        pos = [(s, c) for s in range(TPB) for c in range(NCH) if (s, c) not in gpos]
+        pairs = [pos[k : k + 2] for k in range(0, len(pos), 2)]
+        gst = {}
+        bst = {}
+
+        def stage_pair(pair):
+            for s, c in pair:
+                gst[(s, c)] = stage(gam[s], c)
+            for s, c in pair:
+                bst[(s, c)] = stage(bet[s], c)
+
+        def b1(b, s, c):
+            t = o[b * TPB + s]
+            nc.vector.scalar_tensor_tensor(out=t[:, cols(c)], in0=t[:, cols(c)], scalar=nmean[b][:, 0:1],
+                                           in1=gst[(s, c)][:], op0=ALU.add, op1=ALU.mult)
+
+        def b2(b, s, c):
+            i = b * TPB + s
+            nc.vector.scalar_tensor_tensor(out=o[i][:, cols(c)], in0=o[i][:, cols(c)], scalar=rstd[b][:, 0:1],
+                                           in1=bst[(s, c)][:], op0=ALU.mult, op1=ALU.add)
+            nc.sync.dma_start(out=out_v[i][:, cols(c)], in_=o[i][:, cols(c)])
+
+        stage_pair(pairs[0])
+        chain_a(1)
+        for k in range(len(pairs)):
+            pair = pairs[k]
+            if k + 1 < len(pairs):
+                stage_pair(pairs[k + 1])
+            if k == 0:
+                for s, c in pair:
+                    b1(0, s, c)
+                for s, c in pair:
+                    b2(0, s, c)
+                for s, c in pair:
+                    b1(1, s, c)
+                chain_b(1)
+                g_phase2(1)
+                for s, c in pair:
+                    b2(1, s, c)
+            else:
+                for b in range(2):
+                    for s, c in pair:
+                        b1(b, s, c)
+                for b in range(2):
+                    for s, c in pair:
+                        b2(b, s, c)
+        for b in range(2):
+            for s, lo, hi in GSL:
+                i = b * TPB + s
+                nc.scalar.dma_start(out=out_v[i][:, lo:hi], in_=o[i][:, lo:hi])

@@ -167,10 +167,10 @@ def tile_multiheadattn_pb_kernel(
         def v_first(u):
             i, c = u // NCH, u % NCH
             if u in VUNITS:
-                nc.vector.tensor_tensor(out=o[i][:, cols(c)], in0=acc[u][:], in1=bo_t[i][:, cols(c)], op=ALU.add)
+                nc.vector.tensor_tensor(out=o[i][:, cols(c)], in0=bo_t[i][:, cols(c)], in1=acc[u][:], op=ALU.add)
             else:
                 nc.vector.scalar_tensor_tensor(
-                    out=o[i][:, cols(c)], in0=acc[u][:], scalar=1.0, in1=o[i][:, cols(c)],
+                    out=o[i][:, cols(c)], in0=o[i][:, cols(c)], scalar=1.0, in1=acc[u][:],
                     op0=ALU.mult, op1=ALU.add, accum_out=sum_col(u),
                 )
 

@@ -25,8 +25,8 @@ N_NORM = 512 * D
 LN_EPS = 1e-5
 FLOPS = 2 * TOKENS * D * K
 
-VUNITS = (1, 3, 4, 5, 10, 11, 15, 16, 17)
-GSL = ((3, 0, 1536), (2, 1024, 1536))
+VUNITS = (1, 3, 4, 5, 9, 10, 11, 15, 16, 17)
+GSL = ((3, 0, 1536),)
 LOADS = (0, "w1", "w2", 1, 2, 3, 4, "h1", 5, 6, 7)
 GB = (3, 2, 0, 1)
 RING = 7

@@ -25,14 +25,17 @@ N_NORM = 512 * D
 LN_EPS = 1e-5
 FLOPS = 2 * TOKENS * D * K
 
-VUNITS = (1, 3, 4, 5, 9, 10, 11, 15, 16, 17)
-GSL = ((3, 0, 1536),)
-LOADS = (0, "w1", "w2", 1, 2, 3, 4, "h1", 5, 6, 7)
+VUNITS = (10, 11, 16, 17)
+HTILES = (0, 1)
+GSL = ((3, 0, 1536), (2, 1024, 1536))
+FIRST = ("h0", "w0", "hp", 0, "wp", 1, "w1", "w2")
+LOADS = (2, 3, 4, "h1", 5, 6, 7)
 GB = (3, 2, 0, 1)
+GROUPS = (3, 2, 1, 1, 1)
 RING = 7
 AHEAD = 1
 TOT0 = 1
-RECIP0 = 2
+RECIP0 = 3
 WARM = 0
 
 
@@ -105,12 +108,16 @@ def tile_multiheadattn_pb_kernel(
             nc.sync.dma_start(out=bo_t[i][:], in_=bo_v[i])
             nc.sync.dma_start(out=x_t[i][:], in_=x_v[i])
 
-        load_codes(h_codes[0], h_attn_words, 0, TOKENS)
-        load_codes(w_codes[0], Wo_words, 0, 2 * CHUNK)
-        load_planes(h_planes[0], h_attn_scales, 0, TOKENS // 2)
-        load_planes(w_planes, Wo_scales, 0, D)
-        for what in LOADS:
-            if what == "w1":
+        for what in FIRST + LOADS:
+            if what == "h0":
+                load_codes(h_codes[0], h_attn_words, 0, TOKENS)
+            elif what == "w0":
+                load_codes(w_codes[0], Wo_words, 0, 2 * CHUNK)
+            elif what == "hp":
+                load_planes(h_planes[0], h_attn_scales, 0, TOKENS // 2)
+            elif what == "wp":
+                load_planes(w_planes, Wo_scales, 0, D)
+            elif what == "w1":
                 load_codes(w_codes[1], Wo_words, 2 * CHUNK, 4 * CHUNK)
             elif what == "w2":
                 load_codes(w_codes[2], Wo_words, 4 * CHUNK, 6 * CHUNK)
@@ -123,7 +130,11 @@ def tile_multiheadattn_pb_kernel(
             nc.sync.dma_start(out=gam[s][:], in_=gamma_v[s])
             nc.sync.dma_start(out=bet[s][:], in_=beta_v[s])
 
+        for i in HTILES:
+            nc.vector.tensor_tensor(out=o[i][:], in0=bo_t[i][:], in1=x_t[i][:], op=ALU.add)
         for i in range(TILES):
+            if i in HTILES:
+                continue
             runs = []
             for c in range(NCH):
                 if i * NCH + c in VUNITS:
@@ -217,9 +228,10 @@ def tile_multiheadattn_pb_kernel(
                 nc.gpsimd.tensor_tensor(out=t[:, lo:hi], in0=t[:, lo:hi], in1=gam[s][:, lo:hi], op=ALU.mult)
                 nc.gpsimd.tensor_tensor(out=t[:, lo:hi], in0=t[:, lo:hi], in1=bet[s][:, lo:hi], op=ALU.add)
 
-        for w in range(WARM):
+        if WARM:
             wt = ring.tile([P, CHUNK], F32, name="wt", tag="bank")
-            nc.tensor.matmul(out=wt[:, 0:P], lhsT=ident[:], rhs=ident[:], start=True, stop=True)
+            for w in range(WARM):
+                nc.tensor.matmul(out=wt[:, 0:P], lhsT=ident[:], rhs=ident[:], start=True, stop=True)
 
         for u in range(-AHEAD, NU + 2):
             if u + AHEAD < NU:
@@ -242,7 +254,11 @@ def tile_multiheadattn_pb_kernel(
 
         gpos = [(s, c) for s, lo, hi in GSL for c in range(lo // CHUNK, hi // CHUNK)]
         pos = [(s, c) for s in range(TPB) for c in range(NCH) if (s, c) not in gpos]
-        pairs = [pos[k : k + 2] for k in range(0, len(pos), 2)]
+        pairs = []
+        k0 = 0
+        for n in GROUPS:
+            pairs.append(pos[k0 : k0 + n])
+            k0 += n
         gst = {}
         bst = {}
 

@@ -27,16 +27,20 @@ FLOPS = 2 * TOKENS * D * K
 
 VUNITS = (10, 11, 16, 17)
 HTILES = (0, 1)
-GSL = ((3, 0, 1536), (2, 1024, 1536))
+GSL = (((3, 0, 1536, "Q"), (2, 512, 1536, "G")), ((2, 512, 1536, "Q"), (3, 0, 1536, "g")))
 FIRST = ("h0", "w0", "hp", 0, "wp", 1, "w1", "w2")
 LOADS = (2, 3, 4, "h1", 5, 6, 7)
 GB = (3, 2, 0, 1)
-GROUPS = (3, 2, 1, 1, 1)
-RING = 7
+VPOS = ((0, 0), (0, 1), (0, 2), (1, 0), (1, 1), (1, 2), (2, 0))
+RESIDENT = 6
+FSTART = 4
+LATE = 9
+RING = 6
 AHEAD = 1
 TOT0 = 1
 RECIP0 = 3
 WARM = 0
+NSQ = TPB - 1 + NCH
 
 
 def tile_multiheadattn_pb_kernel(
@@ -55,7 +59,7 @@ def tile_multiheadattn_pb_kernel(
     with ExitStack() as ctx:
         keep = ctx.enter_context(tc.tile_pool(name="keep", bufs=1))
         ring = ctx.enter_context(tc.psum_pool(name="ring", bufs=RING))
-        tiny = ctx.enter_context(tc.psum_pool(name="tiny", bufs=1))
+        tiny = ctx.enter_context(tc.psum_pool(name="tiny", bufs=2))
         ctx.enter_context(tc.manual_schedule())
 
         h_codes = [keep.tile([P, PASSES, TOKENS], U8, name="h_codes%d" % b, align_bytes=64) for b in range(2)]
@@ -69,11 +73,12 @@ def tile_multiheadattn_pb_kernel(
         o = [keep.tile([P, D], F32, name="o%d" % i) for i in range(TILES)]
         ident = keep.tile([P, P], BF16, name="ident")
         ones = keep.tile([P, P], F32, name="ones")
+        ident_f = keep.tile([P, P], F32, name="ident_f")
         eps_t = keep.tile([P, 1], F32, name="eps_t")
         warm = keep.tile([P, 1], F32, name="warm")
-        junk = keep.tile([P, CHUNK], BF16, name="junk")
-        junk_s = keep.tile([P, 2 * UNITS], F32, name="junk_s")
-        stat = [keep.tile([P, 2 * UNITS], F32, name="stat%d" % b) for b in range(2)]
+        junk = keep.tile([P, D], BF16, name="junk")
+        junk_s = keep.tile([P, UNITS + NSQ], F32, name="junk_s")
+        stat = [keep.tile([P, UNITS + NSQ], F32, name="stat%d" % b) for b in range(2)]
         negc = [keep.tile([P, 1], F32, name="negc%d" % b) for b in range(2)]
         nmean = [keep.tile([P, 1], F32, name="nmean%d" % b) for b in range(2)]
         qq = [keep.tile([P, 1], F32, name="qq%d" % b) for b in range(2)]
@@ -88,8 +93,9 @@ def tile_multiheadattn_pb_kernel(
         nc.vector.memset(eps_t[:], LN_EPS)
         nc.vector.memset(ones[:], 1.0)
         nc.vector.memset(h_planes[1][:].bitcast(I32), 0)
-        nc.scalar.activation(out=warm[:], in_=eps_t[:], func=ACT.Sqrt)
+        nc.scalar.activation(out=warm[:], in_=eps_t[:], func=ACT.Abs_reciprocal_sqrt)
         make_identity(nc, ident[:])
+        make_identity(nc, ident_f[:])
 
         def load_codes(dst, src, lo, hi):
             nc.sync.dma_start(
@@ -199,34 +205,84 @@ def tile_multiheadattn_pb_kernel(
 
         def s_unit(u):
             i, c = u // NCH, u % NCH
-            b = u // UNITS
-            j = UNITS + u % UNITS
+            b, s = i // TPB, i % TPB
+            if s < TPB - 1:
+                if c < NCH - 1:
+                    return
+                sl = slice(0, D)
+                j = UNITS + s
+            else:
+                sl = cols(c)
+                j = UNITS + s + c
             nc.scalar.activation(
-                out=junk[:], in_=o[i][:, cols(c)], func=ACT.Square, bias=negc[b][:, 0:1], scale=1.0,
+                out=junk[:, sl], in_=o[i][:, sl], func=ACT.Square, bias=negc[b][:, 0:1], scale=1.0,
                 accum_out=stat[b][:, j : j + 1],
             )
 
         def chain_a(b):
-            t = tiny.tile([P, 2 * UNITS], F32, name="tot", tag="tiny")
+            t = tiny.tile([P, UNITS + NSQ], F32, name="tot", tag="tiny")
             nc.tensor.matmul(out=t[:], lhsT=ones[:], rhs=stat[b][:], start=True, stop=True)
             nc.scalar.activation(out=junk_s[:, 0:UNITS], in_=t[:, 0:UNITS], func=ACT.Copy,
                                  scale=-1.0 / N_NORM, accum_out=nmean[b][:])
-            nc.scalar.activation(out=junk_s[:, UNITS : 2 * UNITS], in_=t[:, UNITS : 2 * UNITS], func=ACT.Copy,
+            nc.scalar.activation(out=junk_s[:, UNITS : UNITS + NSQ], in_=t[:, UNITS : UNITS + NSQ], func=ACT.Copy,
                                  scale=1.0 / N_NORM, accum_out=qq[b][:])
             nc.scalar.activation(out=d2[b][:], in_=nmean[b][:], func=ACT.Square, bias=negc[b][:, 0:1], scale=-1.0)
             nc.scalar.activation(out=var[b][:], in_=d2[b][:], func=ACT.Identity, bias=qq[b][:, 0:1], scale=-1.0)
-            nc.scalar.activation(out=std[b][:], in_=var[b][:], func=ACT.Sqrt, bias=eps_t[:, 0:1], scale=1.0)
-
-        def chain_b(b):
-            nc.vector.reciprocal(out=rstd[b][:], in_=std[b][:])
+            nc.scalar.activation(out=rstd[b][:], in_=var[b][:], func=ACT.Abs_reciprocal_sqrt, bias=eps_t[:, 0:1], scale=1.0)
             nc.scalar.activation(out=nmr[b][:], in_=nmean[b][:], func=ACT.Copy, scale=rstd[b][:, 0:1])
 
-        def g_phase2(b):
-            for s, lo, hi in GSL:
-                t = o[b * TPB + s]
-                nc.scalar.activation(out=t[:, lo:hi], in_=t[:, lo:hi], func=ACT.Identity, bias=nmr[b][:, 0:1], scale=rstd[b][:, 0:1])
+        def g_norm(b, e):
+            s, lo, hi, how = GSL[b][e]
+            t = o[b * TPB + s]
+            nc.scalar.activation(out=t[:, lo:hi], in_=t[:, lo:hi], func=ACT.Identity, bias=nmr[b][:, 0:1], scale=rstd[b][:, 0:1])
+
+        def g_ops(b, e):
+            s, lo, hi, how = GSL[b][e]
+            t = o[b * TPB + s]
+            if how == "G":
                 nc.gpsimd.tensor_tensor(out=t[:, lo:hi], in0=t[:, lo:hi], in1=gam[s][:, lo:hi], op=ALU.mult)
                 nc.gpsimd.tensor_tensor(out=t[:, lo:hi], in0=t[:, lo:hi], in1=bet[s][:, lo:hi], op=ALU.add)
+            elif how == "g":
+                nc.gpsimd.tensor_tensor(out=t[:, lo:hi], in0=t[:, lo:hi], in1=gam[s][:, lo:hi], op=ALU.mult)
+                for cc in range(lo // CHUNK, hi // CHUNK):
+                    nc.gpsimd.tensor_tensor(out=t[:, cols(cc)], in0=t[:, cols(cc)], in1=bet[s][:, cols(cc)], op=ALU.add)
+            else:
+                for cc in range(lo // CHUNK, hi // CHUNK):
+                    nc.gpsimd.tensor_tensor(out=t[:, cols(cc)], in0=t[:, cols(cc)], in1=gam[s][:, cols(cc)], op=ALU.mult)
+
+        def g_phase2(b):
+            for e in range(len(GSL[b])):
+                g_norm(b, e)
+                g_ops(b, e)
+
+        def q_fin(b, s, cc):
+            i = b * TPB + s
+            q = tiny.tile([P, CHUNK], F32, name="q", tag="tiny")
+            nc.tensor.matmul(out=q[:], lhsT=ident_f[:], rhs=o[i][:, cols(cc)], start=True, stop=False)
+            nc.tensor.matmul(out=q[:], lhsT=ident[:], rhs=bet[s][:, cols(cc)], start=False, stop=True)
+            nc.scalar.copy(out=o[i][:, cols(cc)], in_=q[:])
+            nc.scalar.dma_start(out=out_v[i][:, cols(cc)], in_=o[i][:, cols(cc)])
+
+        def g_store(b, s, lo, hi):
+            i = b * TPB + s
+            nc.scalar.dma_start(out=out_v[i][:, lo:hi], in_=o[i][:, lo:hi])
+
+        def finish_items(b, e):
+            s, lo, hi, how = GSL[b][e]
+            if how == "Q":
+                return [("q", b, s, cc) for cc in range(lo // CHUNK, hi // CHUNK)]
+            if how == "g":
+                return [("s", b, s, cc * CHUNK, (cc + 1) * CHUNK) for cc in range(lo // CHUNK, hi // CHUNK)]
+            return [("s", b, s, lo, hi)]
+
+        def do_item(it):
+            if it[0] == "q":
+                q_fin(*it[1:])
+            elif it[0] == "s":
+                g_store(*it[1:])
+            else:
+                g_norm(*it[1:])
+                g_ops(*it[1:])
 
         if WARM:
             wt = ring.tile([P, CHUNK], F32, name="wt", tag="bank")
@@ -247,63 +303,50 @@ def tile_multiheadattn_pb_kernel(
             if u - 2 == UNITS - 1 + TOT0:
                 chain_a(0)
             if u - 2 == UNITS - 1 + RECIP0:
-                chain_b(0)
                 g_phase2(0)
             if 0 <= u - 2 < NU:
                 s_unit(u - 2)
 
-        gpos = [(s, c) for s, lo, hi in GSL for c in range(lo // CHUNK, hi // CHUNK)]
-        pos = [(s, c) for s in range(TPB) for c in range(NCH) if (s, c) not in gpos]
-        pairs = []
-        k0 = 0
-        for n in GROUPS:
-            pairs.append(pos[k0 : k0 + n])
-            k0 += n
-        gst = {}
-        bst = {}
+        gb = {}
 
-        def stage_pair(pair):
-            for s, c in pair:
-                gst[(s, c)] = stage(gam[s], c)
-            for s, c in pair:
-                bst[(s, c)] = stage(bet[s], c)
+        def stage_pos(pos):
+            s, c = pos
+            st = ring.tile([P, 2, CHUNK], BF16, name="gb", tag="bank")
+            nc.tensor.matmul(out=st[:, 0, :], lhsT=ident[:], rhs=gam[s][:, cols(c)], start=True, stop=True)
+            nc.tensor.matmul(out=st[:, 1, :], lhsT=ident[:], rhs=bet[s][:, cols(c)], start=True, stop=True)
+            gb[pos] = st
 
-        def b1(b, s, c):
+        def b1(b, pos):
+            s, c = pos
             t = o[b * TPB + s]
             nc.vector.scalar_tensor_tensor(out=t[:, cols(c)], in0=t[:, cols(c)], scalar=nmean[b][:, 0:1],
-                                           in1=gst[(s, c)][:], op0=ALU.add, op1=ALU.mult)
+                                           in1=gb[pos][:, 0, :], op0=ALU.add, op1=ALU.mult)
 
-        def b2(b, s, c):
+        def b2(b, pos):
+            s, c = pos
             i = b * TPB + s
             nc.vector.scalar_tensor_tensor(out=o[i][:, cols(c)], in0=o[i][:, cols(c)], scalar=rstd[b][:, 0:1],
-                                           in1=bst[(s, c)][:], op0=ALU.mult, op1=ALU.add)
+                                           in1=gb[pos][:, 1, :], op0=ALU.mult, op1=ALU.add)
             nc.sync.dma_start(out=out_v[i][:, cols(c)], in_=o[i][:, cols(c)])
 
-        stage_pair(pairs[0])
+        items = finish_items(0, 0)[:1] + [("n", 1, 1)] + finish_items(0, 0)[1:] + finish_items(0, 1) + finish_items(1, 0) + finish_items(1, 1)
+        work = [(0, pos) for pos in VPOS[:RESIDENT]] + [(1, pos) for pos in VPOS[:RESIDENT]] + [(b, pos) for pos in VPOS[RESIDENT:] for b in range(2)]
+
+        for pos in VPOS[:RESIDENT]:
+            stage_pos(pos)
         chain_a(1)
-        for k in range(len(pairs)):
-            pair = pairs[k]
-            if k + 1 < len(pairs):
-                stage_pair(pairs[k + 1])
-            if k == 0:
-                for s, c in pair:
-                    b1(0, s, c)
-                for s, c in pair:
-                    b2(0, s, c)
-                for s, c in pair:
-                    b1(1, s, c)
-                chain_b(1)
-                g_phase2(1)
-                for s, c in pair:
-                    b2(1, s, c)
-            else:
-                for b in range(2):
-                    for s, c in pair:
-                        b1(b, s, c)
-                for b in range(2):
-                    for s, c in pair:
-                        b2(b, s, c)
-        for b in range(2):
-            for s, lo, hi in GSL:
-                i = b * TPB + s
-                nc.scalar.dma_start(out=out_v[i][:, lo:hi], in_=o[i][:, lo:hi])
+        g_norm(1, 0)
+        g_ops(1, 0)
+        for k in range(len(work) + 1):
+            if k == LATE:
+                for pos in VPOS[RESIDENT:]:
+                    stage_pos(pos)
+            if k < len(work):
+                b1(*work[k])
+            if k > 0:
+                b2(*work[k - 1])
+            if k >= FSTART and items:
+                do_item(items[0])
+                items = items[1:]
+        for it in items:
+            do_item(it)

@@ -104,10 +104,10 @@ def tile_multiheadattn_pb_kernel(
             )
 
         def load_planes(dst, src, lo, hi):
-            for q in range(4):
+            for r in range(4):
                 nc.sync.dma_start(
-                    out=dst[32 * q : 32 * q + 4, :, :].bitcast(I32),
-                    in_=src[:, 4 * q : 4 * q + 4, lo:hi].rearrange("g r n -> r g n").bitcast(I32),
+                    out=dst[r : P : 32, :, :].bitcast(I32),
+                    in_=src[:, r : 16 : 4, lo:hi].rearrange("g q n -> q g n").bitcast(I32),
                 )
 
         def load_pair(i):

@@ -26,7 +26,8 @@ LN_EPS = 1e-5
 FLOPS = 2 * TOKENS * D * K
 
 VUNITS = (10, 11, 16, 17)
-HTILES = (0, 1)
+HTILES = (0, 1, 2)
+LATEH = {2: 4}
 GSL = (((3, 0, 1536, "Q"), (2, 512, 1536, "G")), ((2, 512, 1536, "Q"), (3, 0, 1536, "g")))
 FIRST = ("h0", "w0", "hp", 0, "wp", 1, "w1", "w2")
 LOADS = (2, 3, 4, "h1", 5, 6, 7)
@@ -137,7 +138,8 @@ def tile_multiheadattn_pb_kernel(
             nc.sync.dma_start(out=bet[s][:], in_=beta_v[s])
 
         for i in HTILES:
-            nc.vector.tensor_tensor(out=o[i][:], in0=bo_t[i][:], in1=x_t[i][:], op=ALU.add)
+            if i not in LATEH:
+                nc.vector.tensor_tensor(out=o[i][:], in0=bo_t[i][:], in1=x_t[i][:], op=ALU.add)
         for i in range(TILES):
             if i in HTILES:
                 continue
@@ -294,6 +296,10 @@ def tile_multiheadattn_pb_kernel(
                 pe_unit(u + AHEAD)
             if 0 <= u + AHEAD - 1 < NU and u + AHEAD - 1 in VUNITS:
                 xst[u + AHEAD - 1] = stage(x_t[(u + AHEAD - 1) // NCH], (u + AHEAD - 1) % NCH)
+            if u in LATEH.values():
+                for i in LATEH:
+                    if LATEH[i] == u:
+                        nc.vector.tensor_tensor(out=o[i][:], in0=bo_t[i][:], in1=x_t[i][:], op=ALU.add)
             if 0 <= u < NU:
                 v_first(u)
             if 0 <= u - 1 < NU and u - 1 in VUNITS:

@@ -28,7 +28,7 @@ FLOPS = 2 * TOKENS * D * K
 VUNITS = (10, 11, 16, 17)
 HTILES = (0, 1, 2)
 LATEH = {2: 4}
-GSL = (((3, 0, 1536, "Q"), (2, 512, 1536, "G")), ((2, 512, 1536, "Q"), (3, 0, 1536, "g")))
+GSL = (((3, 0, 1536, "Q"), (2, 0, 1536, "G")), ((2, 512, 1536, "Q"), (3, 0, 1536, "g")))
 FIRST = ("h0", "w0", "hp", 0, "wp", 1, "w1", "w2")
 LOADS = (2, 3, 4, "h1", 5, 6, 7)
 GB = (3, 2, 0, 1)
@@ -336,7 +336,7 @@ def tile_multiheadattn_pb_kernel(
             nc.sync.dma_start(out=out_v[i][:, cols(c)], in_=o[i][:, cols(c)])
 
         items = finish_items(0, 0)[:1] + [("n", 1, 1)] + finish_items(0, 0)[1:] + finish_items(0, 1) + finish_items(1, 0) + finish_items(1, 1)
-        work = [(0, pos) for pos in VPOS[:RESIDENT]] + [(1, pos) for pos in VPOS[:RESIDENT]] + [(b, pos) for pos in VPOS[RESIDENT:] for b in range(2)]
+        work = [(0, pos) for pos in VPOS[:RESIDENT]] + [(1, pos) for pos in VPOS[:RESIDENT]] + [(1, pos) for pos in VPOS[RESIDENT:]]
 
         for pos in VPOS[:RESIDENT]:
             stage_pos(pos)

@@ -28,7 +28,7 @@ FLOPS = 2 * TOKENS * D * K
 VUNITS = (10, 11, 16, 17)
 HTILES = (0, 1, 2)
 LATEH = {2: 4}
-GSL = (((3, 0, 1536, "Q"), (2, 0, 1536, "G")), ((2, 512, 1536, "Q"), (3, 0, 1536, "g")))
+GSL = (((3, 0, 512, "Q"), (3, 512, 1536, "G"), (2, 0, 1536, "G")), ((2, 512, 1536, "Q"), (3, 0, 1024, "Q"), (3, 1024, 1536, "g")))
 FIRST = ("h0", "w0", "hp", 0, "wp", 1, "w1", "w2")
 LOADS = (2, 3, 4, "h1", 5, 6, 7)
 GB = (3, 2, 0, 1)
@@ -335,7 +335,7 @@ def tile_multiheadattn_pb_kernel(
                                            in1=gb[pos][:, 1, :], op0=ALU.mult, op1=ALU.add)
             nc.sync.dma_start(out=out_v[i][:, cols(c)], in_=o[i][:, cols(c)])
 
-        items = finish_items(0, 0)[:1] + [("n", 1, 1)] + finish_items(0, 0)[1:] + finish_items(0, 1) + finish_items(1, 0) + finish_items(1, 1)
+        items = finish_items(0, 0) + [("n", 1, 1), ("n", 1, 2)] + finish_items(0, 1) + finish_items(0, 2) + finish_items(1, 0) + finish_items(1, 1) + finish_items(1, 2)
         work = [(0, pos) for pos in VPOS[:RESIDENT]] + [(1, pos) for pos in VPOS[:RESIDENT]] + [(1, pos) for pos in VPOS[RESIDENT:]]
 
         for pos in VPOS[:RESIDENT]:

@@ -17,31 +17,32 @@ D = 1536
 K = 1536
 PASSES = K // 512
 CHUNK = 512
-NCH = D // CHUNK
+CHUNKS = D // CHUNK
 TILES = TOKENS // P
-TPB = TILES // 2
-UNITS = TPB * NCH
-N_NORM = 512 * D
+BATCH_TILES = TILES // 2
+BATCH_UNITS = BATCH_TILES * CHUNKS
+ALL_UNITS = TILES * CHUNKS
+N_NORM = BATCH_TILES * P * D
 LN_EPS = 1e-5
 FLOPS = 2 * TOKENS * D * K
 
-VUNITS = (10, 11, 16, 17)
-HTILES = (0, 1, 2)
-LATEH = {2: 4}
-GSL = (((3, 0, 512, "Q"), (3, 512, 1536, "G"), (2, 0, 1536, "G")), ((2, 512, 1536, "Q"), (3, 0, 1024, "Q"), (3, 1024, 1536, "g")))
-FIRST = ("h0", "w0", "hp", 0, "wp", 1, "w1", "w2")
-LOADS = (2, 3, 4, "h1", 5, 6, 7)
-GB = (3, 2, 0, 1)
-VPOS = ((0, 0), (0, 1), (0, 2), (1, 0), (1, 1), (1, 2), (2, 0))
-RESIDENT = 6
-FSTART = 4
-LATE = 9
-RING = 6
-AHEAD = 1
-TOT0 = 1
-RECIP0 = 3
-WARM = 0
-NSQ = TPB - 1 + NCH
+SQUARE_COLUMNS = BATCH_TILES - 1 + CHUNKS
+
+VECTOR_SUM_TILES = (0, 1, 2)
+TILE_2_SUM_BEFORE_UNIT = 4
+PSUM_X_TILES = (3, 5)
+
+GPSIMD_SHARE = (
+    ((3, 0, 512, True), (3, 512, 1536, False), (2, 0, 1536, False)),
+    ((2, 512, 1536, True), (3, 0, 1024, True), (3, 1024, 1536, False)),
+)
+VECTOR_POSITIONS = ((0, 0), (0, 1), (0, 2), (1, 0), (1, 1), (1, 2))
+VECTOR_EXTRA_POSITION = (2, 0)
+STAGE_EXTRA_AT_ITEM = 9
+WEAVE_FROM_ITEM = 4
+
+PRODUCT_BANKS = 6
+SMALL_BANKS = 2
 
 
 def tile_multiheadattn_pb_kernel(
@@ -57,46 +58,48 @@ def tile_multiheadattn_pb_kernel(
     def cols(c):
         return slice(c * CHUNK, (c + 1) * CHUNK)
 
+    def x_from_psum(u):
+        return 0 <= u < ALL_UNITS and u // CHUNKS in PSUM_X_TILES and u % CHUNKS > 0
+
     with ExitStack() as ctx:
         keep = ctx.enter_context(tc.tile_pool(name="keep", bufs=1))
-        ring = ctx.enter_context(tc.psum_pool(name="ring", bufs=RING))
-        tiny = ctx.enter_context(tc.psum_pool(name="tiny", bufs=2))
+        banks = ctx.enter_context(tc.psum_pool(name="banks", bufs=PRODUCT_BANKS))
+        small = ctx.enter_context(tc.psum_pool(name="small", bufs=SMALL_BANKS))
         ctx.enter_context(tc.manual_schedule())
 
         h_codes = [keep.tile([P, PASSES, TOKENS], U8, name="h_codes%d" % b, align_bytes=64) for b in range(2)]
         h_planes = [keep.tile([P, PASSES, TOKENS // 2], U8, name="h_planes%d" % b, align_bytes=64) for b in range(2)]
-        w_codes = [keep.tile([P, PASSES, 2 * CHUNK], U8, name="w_codes%d" % c, align_bytes=64) for c in range(NCH)]
+        w_codes = [keep.tile([P, PASSES, 2 * CHUNK], U8, name="w_codes%d" % c, align_bytes=64) for c in range(CHUNKS)]
         w_planes = keep.tile([P, PASSES, D], U8, name="w_planes", align_bytes=64)
         bo_t = [keep.tile([P, D], BF16, name="bo_t%d" % i) for i in range(TILES)]
         x_t = [keep.tile([P, D], BF16, name="x_t%d" % i) for i in range(TILES)]
-        gam = [keep.tile([P, D], BF16, name="gam%d" % s) for s in range(TPB)]
-        bet = [keep.tile([P, D], BF16, name="bet%d" % s) for s in range(TPB)]
+        gamma_t = [keep.tile([P, D], BF16, name="gamma_t%d" % s) for s in range(BATCH_TILES)]
+        beta_t = [keep.tile([P, D], BF16, name="beta_t%d" % s) for s in range(BATCH_TILES)]
         o = [keep.tile([P, D], F32, name="o%d" % i) for i in range(TILES)]
         ident = keep.tile([P, P], BF16, name="ident")
         ones = keep.tile([P, P], F32, name="ones")
-        ident_f = keep.tile([P, P], F32, name="ident_f")
-        eps_t = keep.tile([P, 1], F32, name="eps_t")
-        warm = keep.tile([P, 1], F32, name="warm")
-        junk = keep.tile([P, D], BF16, name="junk")
-        junk_s = keep.tile([P, UNITS + NSQ], F32, name="junk_s")
-        stat = [keep.tile([P, UNITS + NSQ], F32, name="stat%d" % b) for b in range(2)]
-        negc = [keep.tile([P, 1], F32, name="negc%d" % b) for b in range(2)]
-        nmean = [keep.tile([P, 1], F32, name="nmean%d" % b) for b in range(2)]
-        qq = [keep.tile([P, 1], F32, name="qq%d" % b) for b in range(2)]
-        d2 = [keep.tile([P, 1], F32, name="d2%d" % b) for b in range(2)]
+        ident_f32 = keep.tile([P, P], F32, name="ident_f32")
+        eps = keep.tile([P, 1], F32, name="eps")
+        table_warmer = keep.tile([P, 1], F32, name="table_warmer")
+        unused_wide = keep.tile([P, D], BF16, name="unused_wide")
+        unused_small = keep.tile([P, BATCH_UNITS + SQUARE_COLUMNS], F32, name="unused_small")
+        sums = [keep.tile([P, BATCH_UNITS + SQUARE_COLUMNS], F32, name="sums%d" % b) for b in range(2)]
+        neg_shift = [keep.tile([P, 1], F32, name="neg_shift%d" % b) for b in range(2)]
+        neg_mean = [keep.tile([P, 1], F32, name="neg_mean%d" % b) for b in range(2)]
+        mean_sq = [keep.tile([P, 1], F32, name="mean_sq%d" % b) for b in range(2)]
+        gap_sq = [keep.tile([P, 1], F32, name="gap_sq%d" % b) for b in range(2)]
         var = [keep.tile([P, 1], F32, name="var%d" % b) for b in range(2)]
-        std = [keep.tile([P, 1], F32, name="std%d" % b) for b in range(2)]
         rstd = [keep.tile([P, 1], F32, name="rstd%d" % b) for b in range(2)]
-        nmr = [keep.tile([P, 1], F32, name="nmr%d" % b) for b in range(2)]
+        neg_mean_rstd = [keep.tile([P, 1], F32, name="neg_mean_rstd%d" % b) for b in range(2)]
 
         nc.vector.memset(h_planes[0][:].bitcast(I32), 0)
         nc.vector.memset(w_planes[:].bitcast(I32), 0)
-        nc.vector.memset(eps_t[:], LN_EPS)
+        nc.vector.memset(eps[:], LN_EPS)
         nc.vector.memset(ones[:], 1.0)
         nc.vector.memset(h_planes[1][:].bitcast(I32), 0)
-        nc.scalar.activation(out=warm[:], in_=eps_t[:], func=ACT.Abs_reciprocal_sqrt)
+        nc.scalar.activation(out=table_warmer[:], in_=eps[:], func=ACT.Abs_reciprocal_sqrt)
         make_identity(nc, ident[:])
-        make_identity(nc, ident_f[:])
+        make_identity(nc, ident_f32[:])
 
         def load_codes(dst, src, lo, hi):
             nc.sync.dma_start(
@@ -111,66 +114,48 @@ def tile_multiheadattn_pb_kernel(
                     in_=src[:, r : 16 : 4, lo:hi].rearrange("g q n -> q g n").bitcast(I32),
                 )
 
-        def load_pair(i):
+        def load_bo_x(i):
             nc.sync.dma_start(out=bo_t[i][:], in_=bo_v[i])
             nc.sync.dma_start(out=x_t[i][:], in_=x_v[i])
 
-        for what in FIRST + LOADS:
-            if what == "h0":
-                load_codes(h_codes[0], h_attn_words, 0, TOKENS)
-            elif what == "w0":
-                load_codes(w_codes[0], Wo_words, 0, 2 * CHUNK)
-            elif what == "hp":
-                load_planes(h_planes[0], h_attn_scales, 0, TOKENS // 2)
-            elif what == "wp":
-                load_planes(w_planes, Wo_scales, 0, D)
-            elif what == "w1":
-                load_codes(w_codes[1], Wo_words, 2 * CHUNK, 4 * CHUNK)
-            elif what == "w2":
-                load_codes(w_codes[2], Wo_words, 4 * CHUNK, 6 * CHUNK)
-            elif what == "h1":
-                load_codes(h_codes[1], h_attn_words, TOKENS, 2 * TOKENS)
-                load_planes(h_planes[1], h_attn_scales, TOKENS // 2, TOKENS)
-            else:
-                load_pair(what)
-        for s in GB:
-            nc.sync.dma_start(out=gam[s][:], in_=gamma_v[s])
-            nc.sync.dma_start(out=bet[s][:], in_=beta_v[s])
+        load_codes(h_codes[0], h_attn_words, 0, TOKENS)
+        load_codes(w_codes[0], Wo_words, 0, 2 * CHUNK)
+        load_planes(h_planes[0], h_attn_scales, 0, TOKENS // 2)
+        load_bo_x(0)
+        load_planes(w_planes, Wo_scales, 0, D)
+        load_bo_x(1)
+        load_codes(w_codes[1], Wo_words, 2 * CHUNK, 4 * CHUNK)
+        load_codes(w_codes[2], Wo_words, 4 * CHUNK, 6 * CHUNK)
+        for i in (2, 3, 4):
+            load_bo_x(i)
+        load_codes(h_codes[1], h_attn_words, TOKENS, 2 * TOKENS)
+        load_planes(h_planes[1], h_attn_scales, TOKENS // 2, TOKENS)
+        for i in (5, 6, 7):
+            load_bo_x(i)
+        for s in (3, 2, 0, 1):
+            nc.sync.dma_start(out=gamma_t[s][:], in_=gamma_v[s])
+            nc.sync.dma_start(out=beta_t[s][:], in_=beta_v[s])
 
-        for i in HTILES:
-            if i not in LATEH:
-                nc.vector.tensor_tensor(out=o[i][:], in0=bo_t[i][:], in1=x_t[i][:], op=ALU.add)
+        def vector_sum(i):
+            nc.vector.tensor_tensor(out=o[i][:], in0=bo_t[i][:], in1=x_t[i][:], op=ALU.add)
+
+        vector_sum(0)
+        vector_sum(1)
         for i in range(TILES):
-            if i in HTILES:
-                continue
-            runs = []
-            for c in range(NCH):
-                if i * NCH + c in VUNITS:
-                    continue
-                if runs and runs[-1][1] == c and i > 0:
-                    runs[-1][1] = c + 1
-                else:
-                    runs.append([c, c + 1])
-            for lo, hi in runs:
-                sl = slice(lo * CHUNK, hi * CHUNK)
-                nc.gpsimd.tensor_tensor(out=o[i][:, sl], in0=bo_t[i][:, sl], in1=x_t[i][:, sl], op=ALU.add)
+            if i not in VECTOR_SUM_TILES:
+                width = CHUNK if i in PSUM_X_TILES else D
+                nc.gpsimd.tensor_tensor(out=o[i][:, 0:width], in0=bo_t[i][:, 0:width], in1=x_t[i][:, 0:width], op=ALU.add)
 
-        acc = {}
-        xst = {}
-        NU = TILES * NCH
+        products = {}
+        x_copies = {}
 
-        def stage(src, c):
-            st = ring.tile([P, CHUNK], F32, name="st", tag="bank")
-            nc.tensor.matmul(out=st[:], lhsT=ident[:], rhs=src[:, cols(c)], start=True, stop=True)
-            return st
-
-        def pe_unit(u):
-            i, c = u // NCH, u % NCH
-            b, s = i // TPB, i % TPB
-            a = ring.tile([P, CHUNK], F32, name="acc", tag="bank")
+        def multiply(u):
+            i, c = u // CHUNKS, u % CHUNKS
+            b, s = i // BATCH_TILES, i % BATCH_TILES
+            bank = banks.tile([P, CHUNK], F32, name="products", tag="bank")
             for g in range(PASSES):
                 nc.tensor.matmul_mx(
-                    out=a[:],
+                    out=bank[:],
                     lhsT=h_codes[b][:, g, 2 * P * s : 2 * P * (s + 1)].bitcast(FP4X4),
                     lhsT_scale=h_planes[b][:, g, P * s : P * (s + 1)],
                     rhs=w_codes[c][:, g, :].bitcast(FP4X4),
@@ -178,181 +163,163 @@ def tile_multiheadattn_pb_kernel(
                     start=(g == 0),
                     stop=(g == PASSES - 1),
                 )
-            acc[u] = a
+            products[u] = bank
 
-        def sum_col(u):
-            return stat[u // UNITS][:, u % UNITS : u % UNITS + 1]
+        def copy_x_to_psum(u):
+            bank = banks.tile([P, CHUNK], F32, name="x_copy", tag="bank")
+            nc.tensor.matmul(out=bank[:], lhsT=ident[:], rhs=x_t[u // CHUNKS][:, cols(u % CHUNKS)], start=True, stop=True)
+            x_copies[u] = bank
 
-        def v_first(u):
-            i, c = u // NCH, u % NCH
-            if u in VUNITS:
-                nc.vector.tensor_tensor(out=o[i][:, cols(c)], in0=bo_t[i][:, cols(c)], in1=acc[u][:], op=ALU.add)
+        def sum_column(u):
+            return sums[u // BATCH_UNITS][:, u % BATCH_UNITS : u % BATCH_UNITS + 1]
+
+        def add_products(u):
+            i, c = u // CHUNKS, u % CHUNKS
+            if x_from_psum(u):
+                nc.vector.tensor_tensor(out=o[i][:, cols(c)], in0=bo_t[i][:, cols(c)], in1=products[u][:], op=ALU.add)
             else:
                 nc.vector.scalar_tensor_tensor(
-                    out=o[i][:, cols(c)], in0=o[i][:, cols(c)], scalar=1.0, in1=acc[u][:],
-                    op0=ALU.mult, op1=ALU.add, accum_out=sum_col(u),
+                    out=o[i][:, cols(c)], in0=o[i][:, cols(c)], scalar=1.0, in1=products[u][:],
+                    op0=ALU.mult, op1=ALU.add, accum_out=sum_column(u),
                 )
 
-        def v_second(u):
-            i, c = u // NCH, u % NCH
+        def add_x_copy(u):
+            i, c = u // CHUNKS, u % CHUNKS
             nc.vector.scalar_tensor_tensor(
-                out=o[i][:, cols(c)], in0=o[i][:, cols(c)], scalar=1.0, in1=xst[u][:],
-                op0=ALU.mult, op1=ALU.add, accum_out=sum_col(u),
+                out=o[i][:, cols(c)], in0=o[i][:, cols(c)], scalar=1.0, in1=x_copies[u][:],
+                op0=ALU.mult, op1=ALU.add, accum_out=sum_column(u),
             )
 
-        def shift(b):
-            t = tiny.tile([P, 1], F32, name="cs", tag="tiny")
-            nc.tensor.matmul(out=t[:], lhsT=ones[:], rhs=stat[b][:, 0:1], start=True, stop=True)
-            nc.scalar.activation(out=negc[b][:], in_=t[:], func=ACT.Copy, scale=-1.0 / (P * CHUNK))
+        def take_shift(b):
+            total = small.tile([P, 1], F32, name="first_sum", tag="small")
+            nc.tensor.matmul(out=total[:], lhsT=ones[:], rhs=sums[b][:, 0:1], start=True, stop=True)
+            nc.scalar.activation(out=neg_shift[b][:], in_=total[:], func=ACT.Copy, scale=-1.0 / (P * CHUNK))
 
-        def s_unit(u):
-            i, c = u // NCH, u % NCH
-            b, s = i // TPB, i % TPB
-            if s < TPB - 1:
-                if c < NCH - 1:
+        def square(u):
+            i, c = u // CHUNKS, u % CHUNKS
+            b, s = i // BATCH_TILES, i % BATCH_TILES
+            if s < BATCH_TILES - 1:
+                if c < CHUNKS - 1:
                     return
-                sl = slice(0, D)
-                j = UNITS + s
+                span = slice(0, D)
+                column = BATCH_UNITS + s
             else:
-                sl = cols(c)
-                j = UNITS + s + c
+                span = cols(c)
+                column = BATCH_UNITS + s + c
             nc.scalar.activation(
-                out=junk[:, sl], in_=o[i][:, sl], func=ACT.Square, bias=negc[b][:, 0:1], scale=1.0,
-                accum_out=stat[b][:, j : j + 1],
+                out=unused_wide[:, span], in_=o[i][:, span], func=ACT.Square, bias=neg_shift[b][:, 0:1], scale=1.0,
+                accum_out=sums[b][:, column : column + 1],
             )
 
-        def chain_a(b):
-            t = tiny.tile([P, UNITS + NSQ], F32, name="tot", tag="tiny")
-            nc.tensor.matmul(out=t[:], lhsT=ones[:], rhs=stat[b][:], start=True, stop=True)
-            nc.scalar.activation(out=junk_s[:, 0:UNITS], in_=t[:, 0:UNITS], func=ACT.Copy,
-                                 scale=-1.0 / N_NORM, accum_out=nmean[b][:])
-            nc.scalar.activation(out=junk_s[:, UNITS : UNITS + NSQ], in_=t[:, UNITS : UNITS + NSQ], func=ACT.Copy,
-                                 scale=1.0 / N_NORM, accum_out=qq[b][:])
-            nc.scalar.activation(out=d2[b][:], in_=nmean[b][:], func=ACT.Square, bias=negc[b][:, 0:1], scale=-1.0)
-            nc.scalar.activation(out=var[b][:], in_=d2[b][:], func=ACT.Identity, bias=qq[b][:, 0:1], scale=-1.0)
-            nc.scalar.activation(out=rstd[b][:], in_=var[b][:], func=ACT.Abs_reciprocal_sqrt, bias=eps_t[:, 0:1], scale=1.0)
-            nc.scalar.activation(out=nmr[b][:], in_=nmean[b][:], func=ACT.Copy, scale=rstd[b][:, 0:1])
+        def statistics(b):
+            totals = small.tile([P, BATCH_UNITS + SQUARE_COLUMNS], F32, name="totals", tag="small")
+            nc.tensor.matmul(out=totals[:], lhsT=ones[:], rhs=sums[b][:], start=True, stop=True)
+            nc.scalar.activation(out=unused_small[:, 0:BATCH_UNITS], in_=totals[:, 0:BATCH_UNITS], func=ACT.Copy,
+                                 scale=-1.0 / N_NORM, accum_out=neg_mean[b][:])
+            nc.scalar.activation(out=unused_small[:, BATCH_UNITS:], in_=totals[:, BATCH_UNITS:], func=ACT.Copy,
+                                 scale=1.0 / N_NORM, accum_out=mean_sq[b][:])
+            nc.scalar.activation(out=gap_sq[b][:], in_=neg_mean[b][:], func=ACT.Square, bias=neg_shift[b][:, 0:1], scale=-1.0)
+            nc.scalar.activation(out=var[b][:], in_=gap_sq[b][:], func=ACT.Identity, bias=mean_sq[b][:, 0:1], scale=-1.0)
+            nc.scalar.activation(out=rstd[b][:], in_=var[b][:], func=ACT.Abs_reciprocal_sqrt, bias=eps[:, 0:1], scale=1.0)
+            nc.scalar.activation(out=neg_mean_rstd[b][:], in_=neg_mean[b][:], func=ACT.Copy, scale=rstd[b][:, 0:1])
 
-        def g_norm(b, e):
-            s, lo, hi, how = GSL[b][e]
-            t = o[b * TPB + s]
-            nc.scalar.activation(out=t[:, lo:hi], in_=t[:, lo:hi], func=ACT.Identity, bias=nmr[b][:, 0:1], scale=rstd[b][:, 0:1])
-
-        def g_ops(b, e):
-            s, lo, hi, how = GSL[b][e]
-            t = o[b * TPB + s]
-            if how == "G":
-                nc.gpsimd.tensor_tensor(out=t[:, lo:hi], in0=t[:, lo:hi], in1=gam[s][:, lo:hi], op=ALU.mult)
-                nc.gpsimd.tensor_tensor(out=t[:, lo:hi], in0=t[:, lo:hi], in1=bet[s][:, lo:hi], op=ALU.add)
-            elif how == "g":
-                nc.gpsimd.tensor_tensor(out=t[:, lo:hi], in0=t[:, lo:hi], in1=gam[s][:, lo:hi], op=ALU.mult)
-                for cc in range(lo // CHUNK, hi // CHUNK):
-                    nc.gpsimd.tensor_tensor(out=t[:, cols(cc)], in0=t[:, cols(cc)], in1=bet[s][:, cols(cc)], op=ALU.add)
+        def start_entry(b, e):
+            s, lo, hi, tensor_adds_beta = GPSIMD_SHARE[b][e]
+            t = o[b * BATCH_TILES + s]
+            nc.scalar.activation(out=t[:, lo:hi], in_=t[:, lo:hi], func=ACT.Identity,
+                                 bias=neg_mean_rstd[b][:, 0:1], scale=rstd[b][:, 0:1])
+            if tensor_adds_beta:
+                for c in range(lo // CHUNK, hi // CHUNK):
+                    nc.gpsimd.tensor_tensor(out=t[:, cols(c)], in0=t[:, cols(c)], in1=gamma_t[s][:, cols(c)], op=ALU.mult)
             else:
-                for cc in range(lo // CHUNK, hi // CHUNK):
-                    nc.gpsimd.tensor_tensor(out=t[:, cols(cc)], in0=t[:, cols(cc)], in1=gam[s][:, cols(cc)], op=ALU.mult)
+                nc.gpsimd.tensor_tensor(out=t[:, lo:hi], in0=t[:, lo:hi], in1=gamma_t[s][:, lo:hi], op=ALU.mult)
+                nc.gpsimd.tensor_tensor(out=t[:, lo:hi], in0=t[:, lo:hi], in1=beta_t[s][:, lo:hi], op=ALU.add)
 
-        def g_phase2(b):
-            for e in range(len(GSL[b])):
-                g_norm(b, e)
-                g_ops(b, e)
-
-        def q_fin(b, s, cc):
-            i = b * TPB + s
-            q = tiny.tile([P, CHUNK], F32, name="q", tag="tiny")
-            nc.tensor.matmul(out=q[:], lhsT=ident_f[:], rhs=o[i][:, cols(cc)], start=True, stop=False)
-            nc.tensor.matmul(out=q[:], lhsT=ident[:], rhs=bet[s][:, cols(cc)], start=False, stop=True)
-            nc.scalar.copy(out=o[i][:, cols(cc)], in_=q[:])
-            nc.scalar.dma_start(out=out_v[i][:, cols(cc)], in_=o[i][:, cols(cc)])
-
-        def g_store(b, s, lo, hi):
-            i = b * TPB + s
+        def finish_columns(b, s, lo, hi, tensor_adds_beta):
+            i = b * BATCH_TILES + s
+            if tensor_adds_beta:
+                bank = small.tile([P, CHUNK], F32, name="with_beta", tag="small")
+                nc.tensor.matmul(out=bank[:], lhsT=ident_f32[:], rhs=o[i][:, lo:hi], start=True, stop=False)
+                nc.tensor.matmul(out=bank[:], lhsT=ident[:], rhs=beta_t[s][:, lo:hi], start=False, stop=True)
+                nc.scalar.copy(out=o[i][:, lo:hi], in_=bank[:])
             nc.scalar.dma_start(out=out_v[i][:, lo:hi], in_=o[i][:, lo:hi])
 
-        def finish_items(b, e):
-            s, lo, hi, how = GSL[b][e]
-            if how == "Q":
-                return [("q", b, s, cc) for cc in range(lo // CHUNK, hi // CHUNK)]
-            if how == "g":
-                return [("s", b, s, cc * CHUNK, (cc + 1) * CHUNK) for cc in range(lo // CHUNK, hi // CHUNK)]
-            return [("s", b, s, lo, hi)]
+        def finish_steps(b, e):
+            s, lo, hi, tensor_adds_beta = GPSIMD_SHARE[b][e]
+            if tensor_adds_beta:
+                return [(finish_columns, (b, s, c * CHUNK, (c + 1) * CHUNK, True)) for c in range(lo // CHUNK, hi // CHUNK)]
+            return [(finish_columns, (b, s, lo, hi, False))]
 
-        def do_item(it):
-            if it[0] == "q":
-                q_fin(*it[1:])
-            elif it[0] == "s":
-                g_store(*it[1:])
-            else:
-                g_norm(*it[1:])
-                g_ops(*it[1:])
+        for u in range(-1, ALL_UNITS + 2):
+            if u + 1 < ALL_UNITS:
+                multiply(u + 1)
+            if x_from_psum(u):
+                copy_x_to_psum(u)
+            if u == TILE_2_SUM_BEFORE_UNIT:
+                vector_sum(2)
+            if 0 <= u < ALL_UNITS:
+                add_products(u)
+            if x_from_psum(u - 1):
+                add_x_copy(u - 1)
+            if u - 1 in (0, BATCH_UNITS):
+                take_shift((u - 1) // BATCH_UNITS)
+            if u - 2 == BATCH_UNITS:
+                statistics(0)
+            if u - 2 == BATCH_UNITS + 2:
+                for e in range(len(GPSIMD_SHARE[0])):
+                    start_entry(0, e)
+            if 0 <= u - 2 < ALL_UNITS:
+                square(u - 2)
 
-        if WARM:
-            wt = ring.tile([P, CHUNK], F32, name="wt", tag="bank")
-            for w in range(WARM):
-                nc.tensor.matmul(out=wt[:, 0:P], lhsT=ident[:], rhs=ident[:], start=True, stop=True)
+        staged = {}
 
-        for u in range(-AHEAD, NU + 2):
-            if u + AHEAD < NU:
-                pe_unit(u + AHEAD)
-            if 0 <= u + AHEAD - 1 < NU and u + AHEAD - 1 in VUNITS:
-                xst[u + AHEAD - 1] = stage(x_t[(u + AHEAD - 1) // NCH], (u + AHEAD - 1) % NCH)
-            if u in LATEH.values():
-                for i in LATEH:
-                    if LATEH[i] == u:
-                        nc.vector.tensor_tensor(out=o[i][:], in0=bo_t[i][:], in1=x_t[i][:], op=ALU.add)
-            if 0 <= u < NU:
-                v_first(u)
-            if 0 <= u - 1 < NU and u - 1 in VUNITS:
-                v_second(u - 1)
-            if u - 1 in (0, UNITS):
-                shift((u - 1) // UNITS)
-            if u - 2 == UNITS - 1 + TOT0:
-                chain_a(0)
-            if u - 2 == UNITS - 1 + RECIP0:
-                g_phase2(0)
-            if 0 <= u - 2 < NU:
-                s_unit(u - 2)
+        def stage_gamma_beta(position):
+            s, c = position
+            bank = banks.tile([P, 2, CHUNK], BF16, name="gamma_beta", tag="bank")
+            nc.tensor.matmul(out=bank[:, 0, :], lhsT=ident[:], rhs=gamma_t[s][:, cols(c)], start=True, stop=True)
+            nc.tensor.matmul(out=bank[:, 1, :], lhsT=ident[:], rhs=beta_t[s][:, cols(c)], start=True, stop=True)
+            staged[position] = bank
 
-        gb = {}
+        def times_gamma(b, position):
+            s, c = position
+            t = o[b * BATCH_TILES + s]
+            nc.vector.scalar_tensor_tensor(out=t[:, cols(c)], in0=t[:, cols(c)], scalar=neg_mean[b][:, 0:1],
+                                           in1=staged[position][:, 0, :], op0=ALU.add, op1=ALU.mult)
 
-        def stage_pos(pos):
-            s, c = pos
-            st = ring.tile([P, 2, CHUNK], BF16, name="gb", tag="bank")
-            nc.tensor.matmul(out=st[:, 0, :], lhsT=ident[:], rhs=gam[s][:, cols(c)], start=True, stop=True)
-            nc.tensor.matmul(out=st[:, 1, :], lhsT=ident[:], rhs=bet[s][:, cols(c)], start=True, stop=True)
-            gb[pos] = st
-
-        def b1(b, pos):
-            s, c = pos
-            t = o[b * TPB + s]
-            nc.vector.scalar_tensor_tensor(out=t[:, cols(c)], in0=t[:, cols(c)], scalar=nmean[b][:, 0:1],
-                                           in1=gb[pos][:, 0, :], op0=ALU.add, op1=ALU.mult)
-
-        def b2(b, pos):
-            s, c = pos
-            i = b * TPB + s
+        def plus_beta_and_store(b, position):
+            s, c = position
+            i = b * BATCH_TILES + s
             nc.vector.scalar_tensor_tensor(out=o[i][:, cols(c)], in0=o[i][:, cols(c)], scalar=rstd[b][:, 0:1],
-                                           in1=gb[pos][:, 1, :], op0=ALU.mult, op1=ALU.add)
+                                           in1=staged[position][:, 1, :], op0=ALU.mult, op1=ALU.add)
             nc.sync.dma_start(out=out_v[i][:, cols(c)], in_=o[i][:, cols(c)])
 
-        items = finish_items(0, 0) + [("n", 1, 1), ("n", 1, 2)] + finish_items(0, 1) + finish_items(0, 2) + finish_items(1, 0) + finish_items(1, 1) + finish_items(1, 2)
-        work = [(0, pos) for pos in VPOS[:RESIDENT]] + [(1, pos) for pos in VPOS[:RESIDENT]] + [(1, pos) for pos in VPOS[RESIDENT:]]
+        items = (
+            [(0, position) for position in VECTOR_POSITIONS]
+            + [(1, position) for position in VECTOR_POSITIONS]
+            + [(1, VECTOR_EXTRA_POSITION)]
+        )
+        woven = (
+            finish_steps(0, 0)
+            + [(start_entry, (1, 1)), (start_entry, (1, 2))]
+            + finish_steps(0, 1)
+            + finish_steps(0, 2)
+            + finish_steps(1, 0)
+            + finish_steps(1, 1)
+            + finish_steps(1, 2)
+        )
+        assert len(woven) == len(items) + 1 - WEAVE_FROM_ITEM
 
-        for pos in VPOS[:RESIDENT]:
-            stage_pos(pos)
-        chain_a(1)
-        g_norm(1, 0)
-        g_ops(1, 0)
-        for k in range(len(work) + 1):
-            if k == LATE:
-                for pos in VPOS[RESIDENT:]:
-                    stage_pos(pos)
-            if k < len(work):
-                b1(*work[k])
+        for position in VECTOR_POSITIONS:
+            stage_gamma_beta(position)
+        statistics(1)
+        start_entry(1, 0)
+        for k in range(len(items) + 1):
+            if k == STAGE_EXTRA_AT_ITEM:
+                stage_gamma_beta(VECTOR_EXTRA_POSITION)
+            if k < len(items):
+                times_gamma(*items[k])
             if k > 0:
-                b2(*work[k - 1])
-            if k >= FSTART and items:
-                do_item(items[0])
-                items = items[1:]
-        for it in items:
-            do_item(it)
+                plus_beta_and_store(*items[k - 1])
+            if k >= WEAVE_FROM_ITEM:
+                step, arguments = woven[k - WEAVE_FROM_ITEM]
+                step(*arguments)

from contextlib import ExitStack

import concourse.mybir as mybir
from concourse.masks import make_identity

F32 = mybir.dt.float32
BF16 = mybir.dt.bfloat16
U8 = mybir.dt.uint8
I32 = mybir.dt.int32
FP4X4 = mybir.dt.float4_e2m1fn_x4
ALU = mybir.AluOpType
ACT = mybir.ActivationFunctionType

P = 128
TOKENS = 1024
D = 1536
K = 1536
PASSES = K // 512
CHUNK = 512
CHUNKS = D // CHUNK
TILES = TOKENS // P
BATCH_TILES = TILES // 2
BATCH_UNITS = BATCH_TILES * CHUNKS
ALL_UNITS = TILES * CHUNKS
N_NORM = BATCH_TILES * P * D
LN_EPS = 1e-5
FLOPS = 2 * TOKENS * D * K

SQUARE_COLUMNS = BATCH_TILES - 1 + CHUNKS

VECTOR_SUM_TILES = (0, 1, 2)
TILE_2_SUM_BEFORE_UNIT = 4
PSUM_X_TILES = (3, 5)

GPSIMD_SHARE = (
    ((3, 0, 512, True), (3, 512, 1536, False), (2, 0, 1536, False)),
    ((2, 512, 1536, True), (3, 0, 1024, True), (3, 1024, 1536, False)),
)
VECTOR_POSITIONS = ((0, 0), (0, 1), (0, 2), (1, 0), (1, 1), (1, 2))
VECTOR_EXTRA_POSITION = (2, 0)
STAGE_EXTRA_AT_ITEM = 9
WEAVE_FROM_ITEM = 4

PRODUCT_BANKS = 6
SMALL_BANKS = 2


def tile_multiheadattn_pb_kernel(
    tc, h_attn_words, h_attn_scales, Wo_words, Wo_scales, bo, x, gamma, beta, out
):
    nc = tc.nc
    bo_v = bo.flatten_outer_dims().rearrange("(i p) d -> i p d", p=P)
    x_v = x.flatten_outer_dims().rearrange("(i p) d -> i p d", p=P)
    out_v = out.flatten_outer_dims().rearrange("(i p) d -> i p d", p=P)
    gamma_v = gamma.rearrange("(s p) d -> s p d", p=P)
    beta_v = beta.rearrange("(s p) d -> s p d", p=P)

    def cols(c):
        return slice(c * CHUNK, (c + 1) * CHUNK)

    def x_from_psum(u):
        return 0 <= u < ALL_UNITS and u // CHUNKS in PSUM_X_TILES and u % CHUNKS > 0

    with ExitStack() as ctx:
        keep = ctx.enter_context(tc.tile_pool(name="keep", bufs=1))
        banks = ctx.enter_context(tc.psum_pool(name="banks", bufs=PRODUCT_BANKS))
        small = ctx.enter_context(tc.psum_pool(name="small", bufs=SMALL_BANKS))
        ctx.enter_context(tc.manual_schedule())

        h_codes = [keep.tile([P, PASSES, TOKENS], U8, name="h_codes%d" % b, align_bytes=64) for b in range(2)]
        h_planes = [keep.tile([P, PASSES, TOKENS // 2], U8, name="h_planes%d" % b, align_bytes=64) for b in range(2)]
        w_codes = [keep.tile([P, PASSES, 2 * CHUNK], U8, name="w_codes%d" % c, align_bytes=64) for c in range(CHUNKS)]
        w_planes = keep.tile([P, PASSES, D], U8, name="w_planes", align_bytes=64)
        bo_t = [keep.tile([P, D], BF16, name="bo_t%d" % i) for i in range(TILES)]
        x_t = [keep.tile([P, D], BF16, name="x_t%d" % i) for i in range(TILES)]
        gamma_t = [keep.tile([P, D], BF16, name="gamma_t%d" % s) for s in range(BATCH_TILES)]
        beta_t = [keep.tile([P, D], BF16, name="beta_t%d" % s) for s in range(BATCH_TILES)]
        o = [keep.tile([P, D], F32, name="o%d" % i) for i in range(TILES)]
        ident = keep.tile([P, P], BF16, name="ident")
        ones = keep.tile([P, P], F32, name="ones")
        ident_f32 = keep.tile([P, P], F32, name="ident_f32")
        eps = keep.tile([P, 1], F32, name="eps")
        table_warmer = keep.tile([P, 1], F32, name="table_warmer")
        unused_wide = keep.tile([P, D], BF16, name="unused_wide")
        unused_small = keep.tile([P, BATCH_UNITS + SQUARE_COLUMNS], F32, name="unused_small")
        sums = [keep.tile([P, BATCH_UNITS + SQUARE_COLUMNS], F32, name="sums%d" % b) for b in range(2)]
        neg_shift = [keep.tile([P, 1], F32, name="neg_shift%d" % b) for b in range(2)]
        neg_mean = [keep.tile([P, 1], F32, name="neg_mean%d" % b) for b in range(2)]
        mean_sq = [keep.tile([P, 1], F32, name="mean_sq%d" % b) for b in range(2)]
        gap_sq = [keep.tile([P, 1], F32, name="gap_sq%d" % b) for b in range(2)]
        var = [keep.tile([P, 1], F32, name="var%d" % b) for b in range(2)]
        rstd = [keep.tile([P, 1], F32, name="rstd%d" % b) for b in range(2)]
        neg_mean_rstd = [keep.tile([P, 1], F32, name="neg_mean_rstd%d" % b) for b in range(2)]

        nc.vector.memset(h_planes[0][:].bitcast(I32), 0)
        nc.vector.memset(w_planes[:].bitcast(I32), 0)
        nc.vector.memset(eps[:], LN_EPS)
        nc.vector.memset(ones[:], 1.0)
        nc.vector.memset(h_planes[1][:].bitcast(I32), 0)
        nc.scalar.activation(out=table_warmer[:], in_=eps[:], func=ACT.Abs_reciprocal_sqrt)
        make_identity(nc, ident[:])
        make_identity(nc, ident_f32[:])

        def load_codes(dst, src, lo, hi):
            nc.sync.dma_start(
                out=dst[:].bitcast(I32),
                in_=src[:, :, lo:hi].rearrange("g p n -> p g n").bitcast(I32),
            )

        def load_planes(dst, src, lo, hi):
            for r in range(4):
                nc.sync.dma_start(
                    out=dst[r : P : 32, :, :].bitcast(I32),
                    in_=src[:, r : 16 : 4, lo:hi].rearrange("g q n -> q g n").bitcast(I32),
                )

        def load_bo_x(i):
            nc.sync.dma_start(out=bo_t[i][:], in_=bo_v[i])
            nc.sync.dma_start(out=x_t[i][:], in_=x_v[i])

        load_codes(h_codes[0], h_attn_words, 0, TOKENS)
        load_codes(w_codes[0], Wo_words, 0, 2 * CHUNK)
        load_planes(h_planes[0], h_attn_scales, 0, TOKENS // 2)
        load_bo_x(0)
        load_planes(w_planes, Wo_scales, 0, D)
        load_bo_x(1)
        load_codes(w_codes[1], Wo_words, 2 * CHUNK, 4 * CHUNK)
        load_codes(w_codes[2], Wo_words, 4 * CHUNK, 6 * CHUNK)
        for i in (2, 3, 4):
            load_bo_x(i)
        load_codes(h_codes[1], h_attn_words, TOKENS, 2 * TOKENS)
        load_planes(h_planes[1], h_attn_scales, TOKENS // 2, TOKENS)
        for i in (5, 6, 7):
            load_bo_x(i)
        for s in (3, 2, 0, 1):
            nc.sync.dma_start(out=gamma_t[s][:], in_=gamma_v[s])
            nc.sync.dma_start(out=beta_t[s][:], in_=beta_v[s])

        def vector_sum(i):
            nc.vector.tensor_tensor(out=o[i][:], in0=bo_t[i][:], in1=x_t[i][:], op=ALU.add)

        vector_sum(0)
        vector_sum(1)
        for i in range(TILES):
            if i not in VECTOR_SUM_TILES:
                width = CHUNK if i in PSUM_X_TILES else D
                nc.gpsimd.tensor_tensor(out=o[i][:, 0:width], in0=bo_t[i][:, 0:width], in1=x_t[i][:, 0:width], op=ALU.add)

        products = {}
        x_copies = {}

        def multiply(u):
            i, c = u // CHUNKS, u % CHUNKS
            b, s = i // BATCH_TILES, i % BATCH_TILES
            bank = banks.tile([P, CHUNK], F32, name="products", tag="bank")
            for g in range(PASSES):
                nc.tensor.matmul_mx(
                    out=bank[:],
                    lhsT=h_codes[b][:, g, 2 * P * s : 2 * P * (s + 1)].bitcast(FP4X4),
                    lhsT_scale=h_planes[b][:, g, P * s : P * (s + 1)],
                    rhs=w_codes[c][:, g, :].bitcast(FP4X4),
                    rhs_scale=w_planes[:, g, cols(c)],
                    start=(g == 0),
                    stop=(g == PASSES - 1),
                )
            products[u] = bank

        def copy_x_to_psum(u):
            bank = banks.tile([P, CHUNK], F32, name="x_copy", tag="bank")
            nc.tensor.matmul(out=bank[:], lhsT=ident[:], rhs=x_t[u // CHUNKS][:, cols(u % CHUNKS)], start=True, stop=True)
            x_copies[u] = bank

        def sum_column(u):
            return sums[u // BATCH_UNITS][:, u % BATCH_UNITS : u % BATCH_UNITS + 1]

        def add_products(u):
            i, c = u // CHUNKS, u % CHUNKS
            if x_from_psum(u):
                nc.vector.tensor_tensor(out=o[i][:, cols(c)], in0=bo_t[i][:, cols(c)], in1=products[u][:], op=ALU.add)
            else:
                nc.vector.scalar_tensor_tensor(
                    out=o[i][:, cols(c)], in0=o[i][:, cols(c)], scalar=1.0, in1=products[u][:],
                    op0=ALU.mult, op1=ALU.add, accum_out=sum_column(u),
                )

        def add_x_copy(u):
            i, c = u // CHUNKS, u % CHUNKS
            nc.vector.scalar_tensor_tensor(
                out=o[i][:, cols(c)], in0=o[i][:, cols(c)], scalar=1.0, in1=x_copies[u][:],
                op0=ALU.mult, op1=ALU.add, accum_out=sum_column(u),
            )

        def take_shift(b):
            total = small.tile([P, 1], F32, name="first_sum", tag="small")
            nc.tensor.matmul(out=total[:], lhsT=ones[:], rhs=sums[b][:, 0:1], start=True, stop=True)
            nc.scalar.activation(out=neg_shift[b][:], in_=total[:], func=ACT.Copy, scale=-1.0 / (P * CHUNK))

        def square(u):
            i, c = u // CHUNKS, u % CHUNKS
            b, s = i // BATCH_TILES, i % BATCH_TILES
            if s < BATCH_TILES - 1:
                if c < CHUNKS - 1:
                    return
                span = slice(0, D)
                column = BATCH_UNITS + s
            else:
                span = cols(c)
                column = BATCH_UNITS + s + c
            nc.scalar.activation(
                out=unused_wide[:, span], in_=o[i][:, span], func=ACT.Square, bias=neg_shift[b][:, 0:1], scale=1.0,
                accum_out=sums[b][:, column : column + 1],
            )

        def statistics(b):
            totals = small.tile([P, BATCH_UNITS + SQUARE_COLUMNS], F32, name="totals", tag="small")
            nc.tensor.matmul(out=totals[:], lhsT=ones[:], rhs=sums[b][:], start=True, stop=True)
            nc.scalar.activation(out=unused_small[:, 0:BATCH_UNITS], in_=totals[:, 0:BATCH_UNITS], func=ACT.Copy,
                                 scale=-1.0 / N_NORM, accum_out=neg_mean[b][:])
            nc.scalar.activation(out=unused_small[:, BATCH_UNITS:], in_=totals[:, BATCH_UNITS:], func=ACT.Copy,
                                 scale=1.0 / N_NORM, accum_out=mean_sq[b][:])
            nc.scalar.activation(out=gap_sq[b][:], in_=neg_mean[b][:], func=ACT.Square, bias=neg_shift[b][:, 0:1], scale=-1.0)
            nc.scalar.activation(out=var[b][:], in_=gap_sq[b][:], func=ACT.Identity, bias=mean_sq[b][:, 0:1], scale=-1.0)
            nc.scalar.activation(out=rstd[b][:], in_=var[b][:], func=ACT.Abs_reciprocal_sqrt, bias=eps[:, 0:1], scale=1.0)
            nc.scalar.activation(out=neg_mean_rstd[b][:], in_=neg_mean[b][:], func=ACT.Copy, scale=rstd[b][:, 0:1])

        def start_entry(b, e):
            s, lo, hi, tensor_adds_beta = GPSIMD_SHARE[b][e]
            t = o[b * BATCH_TILES + s]
            nc.scalar.activation(out=t[:, lo:hi], in_=t[:, lo:hi], func=ACT.Identity,
                                 bias=neg_mean_rstd[b][:, 0:1], scale=rstd[b][:, 0:1])
            if tensor_adds_beta:
                for c in range(lo // CHUNK, hi // CHUNK):
                    nc.gpsimd.tensor_tensor(out=t[:, cols(c)], in0=t[:, cols(c)], in1=gamma_t[s][:, cols(c)], op=ALU.mult)
            else:
                nc.gpsimd.tensor_tensor(out=t[:, lo:hi], in0=t[:, lo:hi], in1=gamma_t[s][:, lo:hi], op=ALU.mult)
                nc.gpsimd.tensor_tensor(out=t[:, lo:hi], in0=t[:, lo:hi], in1=beta_t[s][:, lo:hi], op=ALU.add)

        def finish_columns(b, s, lo, hi, tensor_adds_beta):
            i = b * BATCH_TILES + s
            if tensor_adds_beta:
                bank = small.tile([P, CHUNK], F32, name="with_beta", tag="small")
                nc.tensor.matmul(out=bank[:], lhsT=ident_f32[:], rhs=o[i][:, lo:hi], start=True, stop=False)
                nc.tensor.matmul(out=bank[:], lhsT=ident[:], rhs=beta_t[s][:, lo:hi], start=False, stop=True)
                nc.scalar.copy(out=o[i][:, lo:hi], in_=bank[:])
            nc.scalar.dma_start(out=out_v[i][:, lo:hi], in_=o[i][:, lo:hi])

        def finish_steps(b, e):
            s, lo, hi, tensor_adds_beta = GPSIMD_SHARE[b][e]
            if tensor_adds_beta:
                return [(finish_columns, (b, s, c * CHUNK, (c + 1) * CHUNK, True)) for c in range(lo // CHUNK, hi // CHUNK)]
            return [(finish_columns, (b, s, lo, hi, False))]

        for u in range(-1, ALL_UNITS + 2):
            if u + 1 < ALL_UNITS:
                multiply(u + 1)
            if x_from_psum(u):
                copy_x_to_psum(u)
            if u == TILE_2_SUM_BEFORE_UNIT:
                vector_sum(2)
            if 0 <= u < ALL_UNITS:
                add_products(u)
            if x_from_psum(u - 1):
                add_x_copy(u - 1)
            if u - 1 in (0, BATCH_UNITS):
                take_shift((u - 1) // BATCH_UNITS)
            if u - 2 == BATCH_UNITS:
                statistics(0)
            if u - 2 == BATCH_UNITS + 2:
                for e in range(len(GPSIMD_SHARE[0])):
                    start_entry(0, e)
            if 0 <= u - 2 < ALL_UNITS:
                square(u - 2)

        staged = {}

        def stage_gamma_beta(position):
            s, c = position
            bank = banks.tile([P, 2, CHUNK], BF16, name="gamma_beta", tag="bank")
            nc.tensor.matmul(out=bank[:, 0, :], lhsT=ident[:], rhs=gamma_t[s][:, cols(c)], start=True, stop=True)
            nc.tensor.matmul(out=bank[:, 1, :], lhsT=ident[:], rhs=beta_t[s][:, cols(c)], start=True, stop=True)
            staged[position] = bank

        def times_gamma(b, position):
            s, c = position
            t = o[b * BATCH_TILES + s]
            nc.vector.scalar_tensor_tensor(out=t[:, cols(c)], in0=t[:, cols(c)], scalar=neg_mean[b][:, 0:1],
                                           in1=staged[position][:, 0, :], op0=ALU.add, op1=ALU.mult)

        def plus_beta_and_store(b, position):
            s, c = position
            i = b * BATCH_TILES + s
            nc.vector.scalar_tensor_tensor(out=o[i][:, cols(c)], in0=o[i][:, cols(c)], scalar=rstd[b][:, 0:1],
                                           in1=staged[position][:, 1, :], op0=ALU.mult, op1=ALU.add)
            nc.sync.dma_start(out=out_v[i][:, cols(c)], in_=o[i][:, cols(c)])

        items = (
            [(0, position) for position in VECTOR_POSITIONS]
            + [(1, position) for position in VECTOR_POSITIONS]
            + [(1, VECTOR_EXTRA_POSITION)]
        )
        woven = (
            finish_steps(0, 0)
            + [(start_entry, (1, 1)), (start_entry, (1, 2))]
            + finish_steps(0, 1)
            + finish_steps(0, 2)
            + finish_steps(1, 0)
            + finish_steps(1, 1)
            + finish_steps(1, 2)
        )
        assert len(woven) == len(items) + 1 - WEAVE_FROM_ITEM

        for position in VECTOR_POSITIONS:
            stage_gamma_beta(position)
        statistics(1)
        start_entry(1, 0)
        for k in range(len(items) + 1):
            if k == STAGE_EXTRA_AT_ITEM:
                stage_gamma_beta(VECTOR_EXTRA_POSITION)
            if k < len(items):
                times_gamma(*items[k])
            if k > 0:
                plus_beta_and_store(*items[k - 1])
            if k >= WEAVE_FROM_ITEM:
                step, arguments = woven[k - WEAVE_FROM_ITEM]
                step(*arguments)
